import numpy as np
import ml_dtypes

BF16 = ml_dtypes.bfloat16


def bf(x):
    return np.asarray(x, np.float32).astype(BF16)


def f32(x):
    return np.asarray(x, np.float32)


def f64(x):
    return np.asarray(x).astype(np.float64)


def striped(idx):
    return np.tile(idx.reshape(-1, 16).T, (8, 1))


B, F, M, C, R, N, S = 2, 512, 2048, 256, 1024, 2048, 4096


def setup_inputs():
    return {"x": bf(np.random.standard_normal((B, F, M))), "adj": bf(0.5 * np.random.uniform(size=(M, N))), "w": bf(0.25 * np.random.standard_normal((F, C)) / np.sqrt(F)), "bias": f32(0.2 * np.random.standard_normal((C, 1))), "base": f32(np.random.standard_normal((C, S))), "offs": striped(np.random.permutation(S)[:N])}


def reference(x, adj, w, bias, base, offs):
    idx = offs[:16].T.reshape(-1)
    k = f64(adj) * f64(adj)
    v = np.concatenate([(f64(x)[u].T @ f64(w)).T @ k[:, u * R:(u + 1) * R] for u in range(B)], axis=1) + f64(bias)
    out = f64(base).copy()
    out[:, idx] = np.maximum(v, 0.0) + (np.exp(np.minimum(v, 0.0)) - 1.0)
    return out

@@ -1,0 +1,108 @@
+import concourse.mybir as mybir
+
+FLOPS = 2 * 2 * 512 * 2048 * 256 + 2 * 2048 * 2048 * 256
+
+BF16, F32, U16 = mybir.dt.bfloat16, mybir.dt.float32, mybir.dt.uint16
+ACT = mybir.ActivationFunctionType
+ALU = mybir.AluOpType
+
+P = 128
+BANK = 512
+X_COLS = 512
+ADJ_ROWS = 2
+
+
+def tile_netgraphconvolution_b_kernel(tc, x, adj, w, bias, base, offs, out):
+    nc = tc.nc
+    graphs, feats, nodes = x.shape
+    chans = w.shape[1]
+    entries = adj.shape[1]
+    slots = base.shape[1]
+    feat_blocks, node_blocks, chan_blocks = feats // P, nodes // P, chans // P
+    graph_entries = entries // graphs
+
+    with (
+        tc.tile_pool(name="held", bufs=1) as held,
+        tc.tile_pool(name="adj_ring", bufs=8) as adj_ring,
+        tc.tile_pool(name="elu_ring", bufs=2) as elu_ring,
+        tc.psum_pool(name="support_banks", bufs=4) as support_banks,
+        tc.psum_pool(name="v_banks", bufs=4) as v_banks,
+    ):
+        w_sb = held.tile([P, feat_blocks, chans], BF16, name="w_sb")
+        nc.scalar.dma_start(w_sb[:], w.rearrange("(b p) c -> p b c", p=P))
+
+        bias_sb, minus_bias = [], []
+        for cb in range(chan_blocks):
+            bias_sb.append(held.tile([P, 1], F32, name=f"bias{cb}"))
+            nc.scalar.dma_start(bias_sb[cb][:], bias[cb * P : (cb + 1) * P, :])
+            minus_bias.append(held.tile([P, 1], F32, name=f"minus_bias{cb}"))
+            nc.vector.tensor_scalar_mul(minus_bias[cb][:], bias_sb[cb][:], -1.0)
+
+        x_view = x.rearrange("u (b p) m -> u p b m", p=P)
+        x_sb = {}
+        for u in range(graphs):
+            for q in range(nodes // X_COLS):
+                x_sb[u, q] = held.tile([P, feat_blocks, X_COLS], BF16, name=f"x{u}_{q}")
+                nc.sync.dma_start(x_sb[u, q][:], x_view[u, :, :, q * X_COLS : (q + 1) * X_COLS])
+
+        adj_view = adj.rearrange("(b p) j -> p b j", p=P)
+        squared = {}
+        for u in range(graphs):
+            for g in range(node_blocks // ADJ_ROWS):
+                raw = adj_ring.tile([P, ADJ_ROWS, graph_entries], BF16, name="raw")
+                nc.sync.dma_start(
+                    raw[:],
+                    adj_view[:, g * ADJ_ROWS : (g + 1) * ADJ_ROWS, u * graph_entries : (u + 1) * graph_entries],
+                )
+                squared[u, g] = held.tile([P, ADJ_ROWS, graph_entries], BF16, name=f"squared{u}_{g}")
+                nc.vector.tensor_tensor(squared[u, g][:], raw[:], raw[:], ALU.mult)
+
+        offsets = held.tile([P, entries // 16], U16, name="offsets")
+        nc.sync.dma_start(offsets[:], offs)
+
+        window = []
+        for cb in range(chan_blocks):
+            window.append(held.tile([P, slots], F32, name=f"window{cb}"))
+            nc.sync.dma_start(window[cb][:], base[cb * P : (cb + 1) * P, :])
+
+        support = []
+        for u in range(graphs):
+            support.append(held.tile([P, node_blocks, chans], BF16, name=f"support{u}"))
+            for pair in range(node_blocks // 2):
+                bank = support_banks.tile([P, 2, chans], F32, name="bank")
+                for half in range(2):
+                    q, col = divmod((2 * pair + half) * P, X_COLS)
+                    for fb in range(feat_blocks):
+                        nc.tensor.matmul(
+                            bank[:, half, :],
+                            x_sb[u, q][:, fb, col : col + P],
+                            w_sb[:, fb, :],
+                            start=fb == 0,
+                            stop=fb == feat_blocks - 1,
+                        )
+                nc.scalar.copy(support[u][:, 2 * pair : 2 * pair + 2, :], bank[:])
+
+        for cb in range(chan_blocks):
+            above = held.tile([P, entries], F32, name=f"above{cb}")
+            below = held.tile([P, entries], F32, name=f"below{cb}")
+            for piece in range(entries // BANK):
+                u, col = divmod(piece * BANK, graph_entries)
+                v = v_banks.tile([P, BANK], F32, name="v")
+                for nb in range(node_blocks):
+                    g, row = divmod(nb, ADJ_ROWS)
+                    nc.tensor.matmul(
+                        v[:],
+                        support[u][:, nb, cb * P : (cb + 1) * P],
+                        squared[u, g][:, row, col : col + BANK],
+                        start=nb == 0,
+                        stop=nb == node_blocks - 1,
+                    )
+                cols = slice(piece * BANK, (piece + 1) * BANK)
+                depth = elu_ring.tile([P, BANK], F32, name="depth")
+                nc.scalar.activation(depth[:], v[:], ACT.Relu, bias=minus_bias[cb][:], scale=-1.0)
+                nc.scalar.activation(below[:, cols], depth[:], ACT.Exp, scale=-1.0)
+                nc.scalar.activation(above[:, cols], v[:], ACT.Relu, bias=bias_sb[cb][:])
+                nc.vector.tensor_scalar_add(below[:, cols], below[:, cols], -1.0)
+
+            nc.vector.tensor_tensor(window[cb][:].indirect(offsets[:]), above[:], below[:], ALU.add)
+            nc.sync.dma_start(out[cb * P : (cb + 1) * P, :], window[cb][:])

@@ -10,6 +10,7 @@ P = 128
 BANK = 512
 X_COLS = 512
 ADJ_ROWS = 2
+PIECE_WIDTHS = (512, 512, 512, 256, 128, 128)
 
 
 def tile_netgraphconvolution_b_kernel(tc, x, adj, w, bias, base, offs, out):
@@ -20,6 +21,7 @@ def tile_netgraphconvolution_b_kernel(tc, x, adj, w, bias, base, offs, out):
     slots = base.shape[1]
     feat_blocks, node_blocks, chan_blocks = feats // P, nodes // P, chans // P
     graph_entries = entries // graphs
+    assert sum(PIECE_WIDTHS) == entries and sum(PIECE_WIDTHS[:2]) == graph_entries
 
     with (
         tc.tile_pool(name="held", bufs=1) as held,
@@ -85,24 +87,27 @@ def tile_netgraphconvolution_b_kernel(tc, x, adj, w, bias, base, offs, out):
         for cb in range(chan_blocks):
             above = held.tile([P, entries], F32, name=f"above{cb}")
             below = held.tile([P, entries], F32, name=f"below{cb}")
-            for piece in range(entries // BANK):
-                u, col = divmod(piece * BANK, graph_entries)
-                v = v_banks.tile([P, BANK], F32, name="v")
+            first = 0
+            for width in PIECE_WIDTHS:
+                u, col = divmod(first, graph_entries)
+                v_bank = v_banks.tile([P, BANK], F32, name="v_bank")
+                v = v_bank[:, :width]
                 for nb in range(node_blocks):
                     g, row = divmod(nb, ADJ_ROWS)
                     nc.tensor.matmul(
-                        v[:],
+                        v,
                         support[u][:, nb, cb * P : (cb + 1) * P],
-                        squared[u, g][:, row, col : col + BANK],
+                        squared[u, g][:, row, col : col + width],
                         start=nb == 0,
                         stop=nb == node_blocks - 1,
                     )
-                cols = slice(piece * BANK, (piece + 1) * BANK)
+                cols = slice(first, first + width)
                 depth = elu_ring.tile([P, BANK], F32, name="depth")
-                nc.scalar.activation(depth[:], v[:], ACT.Relu, bias=minus_bias[cb][:], scale=-1.0)
-                nc.scalar.activation(below[:, cols], depth[:], ACT.Exp, scale=-1.0)
-                nc.scalar.activation(above[:, cols], v[:], ACT.Relu, bias=bias_sb[cb][:])
+                nc.scalar.activation(depth[:, :width], v, ACT.Relu, bias=minus_bias[cb][:], scale=-1.0)
+                nc.scalar.activation(below[:, cols], depth[:, :width], ACT.Exp, scale=-1.0)
+                nc.scalar.activation(above[:, cols], v, ACT.Relu, bias=bias_sb[cb][:])
                 nc.vector.tensor_scalar_add(below[:, cols], below[:, cols], -1.0)
+                first += width
 
             nc.vector.tensor_tensor(window[cb][:].indirect(offsets[:]), above[:], below[:], ALU.add)
             nc.sync.dma_start(out[cb * P : (cb + 1) * P, :], window[cb][:])

@@ -11,6 +11,7 @@ BANK = 512
 X_COLS = 512
 ADJ_ROWS = 2
 PIECE_WIDTHS = (512, 512, 512, 256, 128, 128)
+WARM_UP_MATMULS = 6
 
 
 def tile_netgraphconvolution_b_kernel(tc, x, adj, w, bias, base, offs, out):
@@ -66,6 +67,12 @@ def tile_netgraphconvolution_b_kernel(tc, x, adj, w, bias, base, offs, out):
         for cb in range(chan_blocks):
             window.append(held.tile([P, slots], F32, name=f"window{cb}"))
             nc.sync.dma_start(window[cb][:], base[cb * P : (cb + 1) * P, :])
+
+        zeros = held.tile([P, BANK], BF16, name="zeros")
+        nc.gpsimd.memset(zeros[:], 0.0)
+        warm_bank = support_banks.tile([P, BANK], F32, name="warm_bank", tag="bank")
+        for turn in range(WARM_UP_MATMULS):
+            nc.tensor.matmul(warm_bank[:], zeros[:, :P], zeros[:], start=True, stop=True)
 
         support = []
         for u in range(graphs):

@@ -8,10 +8,10 @@ ALU = mybir.AluOpType
 
 P = 128
 BANK = 512
-X_COLS = 512
+X_LOADS = (128, 384, 512, 512, 512)
 ADJ_ROWS = 2
 PIECE_WIDTHS = (512, 512, 512, 256, 128, 128)
-WARM_UP_MATMULS = 6
+WARM_UP_MATMULS = 4
 
 
 def tile_netgraphconvolution_b_kernel(tc, x, adj, w, bias, base, offs, out):
@@ -34,19 +34,21 @@ def tile_netgraphconvolution_b_kernel(tc, x, adj, w, bias, base, offs, out):
         w_sb = held.tile([P, feat_blocks, chans], BF16, name="w_sb")
         nc.scalar.dma_start(w_sb[:], w.rearrange("(b p) c -> p b c", p=P))
 
-        bias_sb, minus_bias = [], []
+        bias_sb = []
         for cb in range(chan_blocks):
             bias_sb.append(held.tile([P, 1], F32, name=f"bias{cb}"))
             nc.scalar.dma_start(bias_sb[cb][:], bias[cb * P : (cb + 1) * P, :])
-            minus_bias.append(held.tile([P, 1], F32, name=f"minus_bias{cb}"))
-            nc.vector.tensor_scalar_mul(minus_bias[cb][:], bias_sb[cb][:], -1.0)
 
         x_view = x.rearrange("u (b p) m -> u p b m", p=P)
-        x_sb = {}
+        x_block = {}
         for u in range(graphs):
-            for q in range(nodes // X_COLS):
-                x_sb[u, q] = held.tile([P, feat_blocks, X_COLS], BF16, name=f"x{u}_{q}")
-                nc.sync.dma_start(x_sb[u, q][:], x_view[u, :, :, q * X_COLS : (q + 1) * X_COLS])
+            start = 0
+            for width in X_LOADS:
+                x_sb = held.tile([P, feat_blocks, width], BF16, name=f"x{u}_{start}")
+                nc.sync.dma_start(x_sb[:], x_view[u, :, :, start : start + width])
+                for nb in range(start // P, (start + width) // P):
+                    x_block[u, nb] = (x_sb, nb * P - start)
+                start += width
 
         adj_view = adj.rearrange("(b p) j -> p b j", p=P)
         squared = {}
@@ -80,11 +82,11 @@ def tile_netgraphconvolution_b_kernel(tc, x, adj, w, bias, base, offs, out):
             for pair in range(node_blocks // 2):
                 bank = support_banks.tile([P, 2, chans], F32, name="bank")
                 for half in range(2):
-                    q, col = divmod((2 * pair + half) * P, X_COLS)
+                    x_sb, col = x_block[u, 2 * pair + half]
                     for fb in range(feat_blocks):
                         nc.tensor.matmul(
                             bank[:, half, :],
-                            x_sb[u, q][:, fb, col : col + P],
+                            x_sb[:, fb, col : col + P],
                             w_sb[:, fb, :],
                             start=fb == 0,
                             stop=fb == feat_blocks - 1,
@@ -109,11 +111,10 @@ def tile_netgraphconvolution_b_kernel(tc, x, adj, w, bias, base, offs, out):
                         stop=nb == node_blocks - 1,
                     )
                 cols = slice(first, first + width)
-                depth = elu_ring.tile([P, BANK], F32, name="depth")
-                nc.scalar.activation(depth[:, :width], v, ACT.Relu, bias=minus_bias[cb][:], scale=-1.0)
-                nc.scalar.activation(below[:, cols], depth[:, :width], ACT.Exp, scale=-1.0)
+                grown = elu_ring.tile([P, BANK], F32, name="grown")
+                nc.scalar.activation(grown[:, :width], v, ACT.Exp, bias=bias_sb[cb][:])
                 nc.scalar.activation(above[:, cols], v, ACT.Relu, bias=bias_sb[cb][:])
-                nc.vector.tensor_scalar_add(below[:, cols], below[:, cols], -1.0)
+                nc.vector.tensor_scalar(below[:, cols], grown[:, :width], 1.0, -1.0, ALU.min, ALU.add)
                 first += width
 
             nc.vector.tensor_tensor(window[cb][:].indirect(offsets[:]), above[:], below[:], ALU.add)

@@ -27,7 +27,6 @@ def tile_netgraphconvolution_b_kernel(tc, x, adj, w, bias, base, offs, out):
     with (
         tc.tile_pool(name="held", bufs=1) as held,
         tc.tile_pool(name="adj_ring", bufs=8) as adj_ring,
-        tc.tile_pool(name="elu_ring", bufs=2) as elu_ring,
         tc.psum_pool(name="support_banks", bufs=4) as support_banks,
         tc.psum_pool(name="v_banks", bufs=4) as v_banks,
     ):
@@ -111,10 +110,9 @@ def tile_netgraphconvolution_b_kernel(tc, x, adj, w, bias, base, offs, out):
                         stop=nb == node_blocks - 1,
                     )
                 cols = slice(first, first + width)
-                grown = elu_ring.tile([P, BANK], F32, name="grown")
-                nc.scalar.activation(grown[:, :width], v, ACT.Exp, bias=bias_sb[cb][:])
+                nc.scalar.activation(below[:, cols], v, ACT.Exp, bias=bias_sb[cb][:])
                 nc.scalar.activation(above[:, cols], v, ACT.Relu, bias=bias_sb[cb][:])
-                nc.vector.tensor_scalar(below[:, cols], grown[:, :width], 1.0, -1.0, ALU.min, ALU.add)
+                nc.vector.tensor_scalar(below[:, cols], below[:, cols], 1.0, -1.0, ALU.min, ALU.add)
                 first += width
 
             nc.vector.tensor_tensor(window[cb][:].indirect(offsets[:]), above[:], below[:], ALU.add)

@@ -9,7 +9,7 @@ ALU = mybir.AluOpType
 P = 128
 BANK = 512
 X_LOADS = (128, 384, 512, 512, 512)
-ADJ_ROWS = 2
+ADJ_ROWS = 4
 PIECE_WIDTHS = (512, 512, 512, 256, 128, 128)
 WARM_UP_MATMULS = 4
 
@@ -22,7 +22,7 @@ def tile_netgraphconvolution_b_kernel(tc, x, adj, w, bias, base, offs, out):
     slots = base.shape[1]
     feat_blocks, node_blocks, chan_blocks = feats // P, nodes // P, chans // P
     graph_entries = entries // graphs
-    assert sum(PIECE_WIDTHS) == entries and sum(PIECE_WIDTHS[:2]) == graph_entries
+    assert sum(PIECE_WIDTHS) == entries and graph_entries % BANK == 0
 
     with (
         tc.tile_pool(name="held", bufs=1) as held,
@@ -51,15 +51,14 @@ def tile_netgraphconvolution_b_kernel(tc, x, adj, w, bias, base, offs, out):
 
         adj_view = adj.rearrange("(b p) j -> p b j", p=P)
         squared = {}
-        for u in range(graphs):
+        for strip in range(entries // BANK):
             for g in range(node_blocks // ADJ_ROWS):
-                raw = adj_ring.tile([P, ADJ_ROWS, graph_entries], BF16, name="raw")
+                raw = adj_ring.tile([P, ADJ_ROWS, BANK], BF16, name="raw")
                 nc.sync.dma_start(
-                    raw[:],
-                    adj_view[:, g * ADJ_ROWS : (g + 1) * ADJ_ROWS, u * graph_entries : (u + 1) * graph_entries],
+                    raw[:], adj_view[:, g * ADJ_ROWS : (g + 1) * ADJ_ROWS, strip * BANK : (strip + 1) * BANK]
                 )
-                squared[u, g] = held.tile([P, ADJ_ROWS, graph_entries], BF16, name=f"squared{u}_{g}")
-                nc.vector.tensor_tensor(squared[u, g][:], raw[:], raw[:], ALU.mult)
+                squared[strip, g] = held.tile([P, ADJ_ROWS, BANK], BF16, name=f"squared{strip}_{g}")
+                nc.vector.tensor_tensor(squared[strip, g][:], raw[:], raw[:], ALU.mult)
 
         offsets = held.tile([P, entries // 16], U16, name="offsets")
         nc.sync.dma_start(offsets[:], offs)
@@ -97,7 +96,9 @@ def tile_netgraphconvolution_b_kernel(tc, x, adj, w, bias, base, offs, out):
             below = held.tile([P, entries], F32, name=f"below{cb}")
             first = 0
             for width in PIECE_WIDTHS:
-                u, col = divmod(first, graph_entries)
+                u = first // graph_entries
+                strip, col = divmod(first, BANK)
+                assert col + width <= BANK
                 v_bank = v_banks.tile([P, BANK], F32, name="v_bank")
                 v = v_bank[:, :width]
                 for nb in range(node_blocks):
@@ -105,7 +106,7 @@ def tile_netgraphconvolution_b_kernel(tc, x, adj, w, bias, base, offs, out):
                     nc.tensor.matmul(
                         v,
                         support[u][:, nb, cb * P : (cb + 1) * P],
-                        squared[u, g][:, row, col : col + width],
+                        squared[strip, g][:, row, col : col + width],
                         start=nb == 0,
                         stop=nb == node_blocks - 1,
                     )

@@ -35,8 +35,10 @@ def tile_netgraphconvolution_b_kernel(tc, x, adj, w, bias, base, offs, out):
 
         bias_sb = []
         for cb in range(chan_blocks):
+            loaded = held.tile([P, 1], F32, name=f"bias_loaded{cb}")
+            nc.scalar.dma_start(loaded[:], bias[cb * P : (cb + 1) * P, :])
             bias_sb.append(held.tile([P, 1], F32, name=f"bias{cb}"))
-            nc.scalar.dma_start(bias_sb[cb][:], bias[cb * P : (cb + 1) * P, :])
+            nc.vector.tensor_copy(bias_sb[cb][:], loaded[:])
 
         x_view = x.rearrange("u (b p) m -> u p b m", p=P)
         x_block = {}
@@ -69,7 +71,7 @@ def tile_netgraphconvolution_b_kernel(tc, x, adj, w, bias, base, offs, out):
             nc.sync.dma_start(window[cb][:], base[cb * P : (cb + 1) * P, :])
 
         zeros = held.tile([P, BANK], BF16, name="zeros")
-        nc.gpsimd.memset(zeros[:], 0.0)
+        nc.vector.memset(zeros[:], 0.0)
         warm_bank = support_banks.tile([P, BANK], F32, name="warm_bank", tag="bank")
         for turn in range(WARM_UP_MATMULS):
             nc.tensor.matmul(warm_bank[:], zeros[:, :P], zeros[:], start=True, stop=True)
@@ -95,7 +97,8 @@ def tile_netgraphconvolution_b_kernel(tc, x, adj, w, bias, base, offs, out):
             above = held.tile([P, entries], F32, name=f"above{cb}")
             below = held.tile([P, entries], F32, name=f"below{cb}")
             first = 0
-            for width in PIECE_WIDTHS:
+            last_block = cb == chan_blocks - 1
+            for width in PIECE_WIDTHS if last_block else (BANK,) * (entries // BANK):
                 u = first // graph_entries
                 strip, col = divmod(first, BANK)
                 assert col + width <= BANK

@@ -33,12 +33,10 @@ def tile_netgraphconvolution_b_kernel(tc, x, adj, w, bias, base, offs, out):
         w_sb = held.tile([P, feat_blocks, chans], BF16, name="w_sb")
         nc.scalar.dma_start(w_sb[:], w.rearrange("(b p) c -> p b c", p=P))
 
-        bias_sb = []
-        for cb in range(chan_blocks):
-            loaded = held.tile([P, 1], F32, name=f"bias_loaded{cb}")
-            nc.scalar.dma_start(loaded[:], bias[cb * P : (cb + 1) * P, :])
-            bias_sb.append(held.tile([P, 1], F32, name=f"bias{cb}"))
-            nc.vector.tensor_copy(bias_sb[cb][:], loaded[:])
+        bias_loaded = held.tile([P, chan_blocks], F32, name="bias_loaded")
+        nc.gpsimd.dma_start(bias_loaded[:], bias.rearrange("(b p) o -> p (b o)", p=P))
+        bias_sb = held.tile([P, chan_blocks], F32, name="bias_sb")
+        nc.vector.tensor_copy(bias_sb[:], bias_loaded[:])
 
         x_view = x.rearrange("u (b p) m -> u p b m", p=P)
         x_block = {}
@@ -114,8 +112,8 @@ def tile_netgraphconvolution_b_kernel(tc, x, adj, w, bias, base, offs, out):
                         stop=nb == node_blocks - 1,
                     )
                 cols = slice(first, first + width)
-                nc.scalar.activation(below[:, cols], v, ACT.Exp, bias=bias_sb[cb][:])
-                nc.scalar.activation(above[:, cols], v, ACT.Relu, bias=bias_sb[cb][:])
+                nc.scalar.activation(below[:, cols], v, ACT.Exp, bias=bias_sb[:, cb : cb + 1])
+                nc.scalar.activation(above[:, cols], v, ACT.Relu, bias=bias_sb[:, cb : cb + 1])
                 nc.vector.tensor_scalar(below[:, cols], below[:, cols], 1.0, -1.0, ALU.min, ALU.add)
                 first += width
 

@@ -7,6 +7,7 @@ ACT = mybir.ActivationFunctionType
 ALU = mybir.AluOpType
 
 P = 128
+ALIGN = 512
 BANK = 512
 X_LOADS = (128, 384, 512, 512, 512)
 ADJ_ROWS = 4
@@ -30,7 +31,7 @@ def tile_netgraphconvolution_b_kernel(tc, x, adj, w, bias, base, offs, out):
         tc.psum_pool(name="support_banks", bufs=4) as support_banks,
         tc.psum_pool(name="v_banks", bufs=4) as v_banks,
     ):
-        w_sb = held.tile([P, feat_blocks, chans], BF16, name="w_sb")
+        w_sb = held.tile([P, feat_blocks, chans], BF16, name="w_sb", align_bytes=ALIGN)
         nc.scalar.dma_start(w_sb[:], w.rearrange("(b p) c -> p b c", p=P))
 
         bias_loaded = held.tile([P, chan_blocks], F32, name="bias_loaded")
@@ -43,7 +44,7 @@ def tile_netgraphconvolution_b_kernel(tc, x, adj, w, bias, base, offs, out):
         for u in range(graphs):
             start = 0
             for width in X_LOADS:
-                x_sb = held.tile([P, feat_blocks, width], BF16, name=f"x{u}_{start}")
+                x_sb = held.tile([P, feat_blocks, width], BF16, name=f"x{u}_{start}", align_bytes=ALIGN)
                 nc.sync.dma_start(x_sb[:], x_view[u, :, :, start : start + width])
                 for nb in range(start // P, (start + width) // P):
                     x_block[u, nb] = (x_sb, nb * P - start)
@@ -53,11 +54,13 @@ def tile_netgraphconvolution_b_kernel(tc, x, adj, w, bias, base, offs, out):
         squared = {}
         for strip in range(entries // BANK):
             for g in range(node_blocks // ADJ_ROWS):
-                raw = adj_ring.tile([P, ADJ_ROWS, BANK], BF16, name="raw")
+                raw = adj_ring.tile([P, ADJ_ROWS, BANK], BF16, name="raw", align_bytes=ALIGN)
                 nc.sync.dma_start(
                     raw[:], adj_view[:, g * ADJ_ROWS : (g + 1) * ADJ_ROWS, strip * BANK : (strip + 1) * BANK]
                 )
-                squared[strip, g] = held.tile([P, ADJ_ROWS, BANK], BF16, name=f"squared{strip}_{g}")
+                squared[strip, g] = held.tile(
+                    [P, ADJ_ROWS, BANK], BF16, name=f"squared{strip}_{g}", align_bytes=ALIGN
+                )
                 nc.vector.tensor_tensor(squared[strip, g][:], raw[:], raw[:], ALU.mult)
 
         offsets = held.tile([P, entries // 16], U16, name="offsets")
@@ -65,10 +68,10 @@ def tile_netgraphconvolution_b_kernel(tc, x, adj, w, bias, base, offs, out):
 
         window = []
         for cb in range(chan_blocks):
-            window.append(held.tile([P, slots], F32, name=f"window{cb}"))
+            window.append(held.tile([P, slots], F32, name=f"window{cb}", align_bytes=ALIGN))
             nc.sync.dma_start(window[cb][:], base[cb * P : (cb + 1) * P, :])
 
-        zeros = held.tile([P, BANK], BF16, name="zeros")
+        zeros = held.tile([P, BANK], BF16, name="zeros", align_bytes=ALIGN)
         nc.vector.memset(zeros[:], 0.0)
         warm_bank = support_banks.tile([P, BANK], F32, name="warm_bank", tag="bank")
         for turn in range(WARM_UP_MATMULS):
@@ -76,7 +79,7 @@ def tile_netgraphconvolution_b_kernel(tc, x, adj, w, bias, base, offs, out):
 
         support = []
         for u in range(graphs):
-            support.append(held.tile([P, node_blocks, chans], BF16, name=f"support{u}"))
+            support.append(held.tile([P, node_blocks, chans], BF16, name=f"support{u}", align_bytes=ALIGN))
             for pair in range(node_blocks // 2):
                 bank = support_banks.tile([P, 2, chans], F32, name="bank")
                 for half in range(2):
@@ -92,8 +95,8 @@ def tile_netgraphconvolution_b_kernel(tc, x, adj, w, bias, base, offs, out):
                 nc.scalar.copy(support[u][:, 2 * pair : 2 * pair + 2, :], bank[:])
 
         for cb in range(chan_blocks):
-            above = held.tile([P, entries], F32, name=f"above{cb}")
-            below = held.tile([P, entries], F32, name=f"below{cb}")
+            above = held.tile([P, entries], F32, name=f"above{cb}", align_bytes=ALIGN)
+            below = held.tile([P, entries], F32, name=f"below{cb}", align_bytes=ALIGN)
             first = 0
             last_block = cb == chan_blocks - 1
             for width in PIECE_WIDTHS if last_block else (BANK,) * (entries // BANK):

@@ -9,10 +9,12 @@ ALU = mybir.AluOpType
 P = 128
 ALIGN = 512
 BANK = 512
-X_LOADS = (128, 384, 512, 512, 512)
+LEAD = 4
+FIRST_LOADS = (slice(0, 1), slice(1, 4))
+X_LOADS = (LEAD * P, 512, 512, 512)
 ADJ_ROWS = 4
-PIECE_WIDTHS = (512, 512, 512, 256, 128, 128)
-WARM_UP_MATMULS = 4
+PIECE_WIDTHS = (512, 512, 512, 256, 128, 64, 64)
+WARM_UP_MATMULS = 3
 
 
 def tile_netgraphconvolution_b_kernel(tc, x, adj, w, bias, base, offs, out):
@@ -28,11 +30,12 @@ def tile_netgraphconvolution_b_kernel(tc, x, adj, w, bias, base, offs, out):
     with (
         tc.tile_pool(name="held", bufs=1) as held,
         tc.tile_pool(name="adj_ring", bufs=8) as adj_ring,
-        tc.psum_pool(name="support_banks", bufs=4) as support_banks,
-        tc.psum_pool(name="v_banks", bufs=4) as v_banks,
+        tc.psum_pool(name="banks", bufs=8) as banks,
     ):
         w_sb = held.tile([P, feat_blocks, chans], BF16, name="w_sb", align_bytes=ALIGN)
-        nc.scalar.dma_start(w_sb[:], w.rearrange("(b p) c -> p b c", p=P))
+        w_view = w.rearrange("(b p) c -> p b c", p=P)
+        for blocks in FIRST_LOADS:
+            nc.scalar.dma_start(w_sb[:, blocks, :], w_view[:, blocks, :])
 
         bias_loaded = held.tile([P, chan_blocks], F32, name="bias_loaded")
         nc.gpsimd.dma_start(bias_loaded[:], bias.rearrange("(b p) o -> p (b o)", p=P))
@@ -45,7 +48,11 @@ def tile_netgraphconvolution_b_kernel(tc, x, adj, w, bias, base, offs, out):
             start = 0
             for width in X_LOADS:
                 x_sb = held.tile([P, feat_blocks, width], BF16, name=f"x{u}_{start}", align_bytes=ALIGN)
-                nc.sync.dma_start(x_sb[:], x_view[u, :, :, start : start + width])
+                if u == 0 and start == 0:
+                    for blocks in FIRST_LOADS:
+                        nc.sync.dma_start(x_sb[:, blocks, :], x_view[u, :, blocks, :width])
+                else:
+                    nc.sync.dma_start(x_sb[:], x_view[u, :, :, start : start + width])
                 for nb in range(start // P, (start + width) // P):
                     x_block[u, nb] = (x_sb, nb * P - start)
                 start += width
@@ -73,15 +80,29 @@ def tile_netgraphconvolution_b_kernel(tc, x, adj, w, bias, base, offs, out):
 
         zeros = held.tile([P, BANK], BF16, name="zeros", align_bytes=ALIGN)
         nc.vector.memset(zeros[:], 0.0)
-        warm_bank = support_banks.tile([P, BANK], F32, name="warm_bank", tag="bank")
+        warm_bank = banks.tile([P, BANK], F32, name="warm_bank", tag="bank")
         for turn in range(WARM_UP_MATMULS):
             nc.tensor.matmul(warm_bank[:], zeros[:, :P], zeros[:], start=True, stop=True)
 
-        support = []
+        support = [
+            held.tile([P, node_blocks, chans], BF16, name=f"support{u}", align_bytes=ALIGN) for u in range(graphs)
+        ]
+        lead_banks = [banks.tile([P, chans], F32, name=f"lead_bank{nb}", tag="bank") for nb in range(LEAD)]
+        for fb in range(feat_blocks):
+            for nb in range(LEAD):
+                x_sb, col = x_block[0, nb]
+                nc.tensor.matmul(
+                    lead_banks[nb][:],
+                    x_sb[:, fb, col : col + P],
+                    w_sb[:, fb, :],
+                    start=fb == 0,
+                    stop=fb == feat_blocks - 1,
+                )
+        for nb in range(LEAD):
+            nc.scalar.copy(support[0][:, nb, :], lead_banks[nb][:])
         for u in range(graphs):
-            support.append(held.tile([P, node_blocks, chans], BF16, name=f"support{u}", align_bytes=ALIGN))
-            for pair in range(node_blocks // 2):
-                bank = support_banks.tile([P, 2, chans], F32, name="bank")
+            for pair in range(LEAD // 2 if u == 0 else 0, node_blocks // 2):
+                bank = banks.tile([P, 2, chans], F32, name="bank", tag="bank")
                 for half in range(2):
                     x_sb, col = x_block[u, 2 * pair + half]
                     for fb in range(feat_blocks):
@@ -103,7 +124,7 @@ def tile_netgraphconvolution_b_kernel(tc, x, adj, w, bias, base, offs, out):
                 u = first // graph_entries
                 strip, col = divmod(first, BANK)
                 assert col + width <= BANK
-                v_bank = v_banks.tile([P, BANK], F32, name="v_bank")
+                v_bank = banks.tile([P, BANK], F32, name="v_bank", tag="bank")
                 v = v_bank[:, :width]
                 for nb in range(node_blocks):
                     g, row = divmod(nb, ADJ_ROWS)

@@ -10,11 +10,12 @@ P = 128
 ALIGN = 512
 BANK = 512
 LEAD = 4
-FIRST_LOADS = (slice(0, 1), slice(1, 4))
-X_LOADS = (LEAD * P, 512, 512, 512)
+W_FIRST = (slice(0, 1), slice(1, 4))
+X_FIRST = (slice(0, 1), slice(1, 2), slice(2, 4))
+X_LOADS = ((LEAD * P, 512, 512, 512), (512, 512, 1024))
 ADJ_ROWS = 4
-PIECE_WIDTHS = (512, 512, 512, 256, 128, 64, 64)
-WARM_UP_MATMULS = 3
+PIECE_WIDTHS = (512, 512, 512, 320, 128, 64)
+WARM_UP_MATMULS = 13
 
 
 def tile_netgraphconvolution_b_kernel(tc, x, adj, w, bias, base, offs, out):
@@ -34,7 +35,7 @@ def tile_netgraphconvolution_b_kernel(tc, x, adj, w, bias, base, offs, out):
     ):
         w_sb = held.tile([P, feat_blocks, chans], BF16, name="w_sb", align_bytes=ALIGN)
         w_view = w.rearrange("(b p) c -> p b c", p=P)
-        for blocks in FIRST_LOADS:
+        for blocks in W_FIRST:
             nc.scalar.dma_start(w_sb[:, blocks, :], w_view[:, blocks, :])
 
         bias_loaded = held.tile([P, chan_blocks], F32, name="bias_loaded")
@@ -46,10 +47,10 @@ def tile_netgraphconvolution_b_kernel(tc, x, adj, w, bias, base, offs, out):
         x_block = {}
         for u in range(graphs):
             start = 0
-            for width in X_LOADS:
+            for width in X_LOADS[u]:
                 x_sb = held.tile([P, feat_blocks, width], BF16, name=f"x{u}_{start}", align_bytes=ALIGN)
                 if u == 0 and start == 0:
-                    for blocks in FIRST_LOADS:
+                    for blocks in X_FIRST:
                         nc.sync.dma_start(x_sb[:, blocks, :], x_view[u, :, blocks, :width])
                 else:
                     nc.sync.dma_start(x_sb[:], x_view[u, :, :, start : start + width])
@@ -78,11 +79,11 @@ def tile_netgraphconvolution_b_kernel(tc, x, adj, w, bias, base, offs, out):
             window.append(held.tile([P, slots], F32, name=f"window{cb}", align_bytes=ALIGN))
             nc.sync.dma_start(window[cb][:], base[cb * P : (cb + 1) * P, :])
 
-        zeros = held.tile([P, BANK], BF16, name="zeros", align_bytes=ALIGN)
+        zeros = held.tile([P, P], BF16, name="zeros", align_bytes=ALIGN)
         nc.vector.memset(zeros[:], 0.0)
-        warm_bank = banks.tile([P, BANK], F32, name="warm_bank", tag="bank")
+        warm_bank = banks.tile([P, P], F32, name="warm_bank", tag="bank")
         for turn in range(WARM_UP_MATMULS):
-            nc.tensor.matmul(warm_bank[:], zeros[:, :P], zeros[:], start=True, stop=True)
+            nc.tensor.matmul(warm_bank[:], zeros[:], zeros[:], start=True, stop=True)
 
         support = [
             held.tile([P, node_blocks, chans], BF16, name=f"support{u}", align_bytes=ALIGN) for u in range(graphs)

@@ -12,7 +12,7 @@ BANK = 512
 LEAD = 4
 W_FIRST = (slice(0, 1), slice(1, 4))
 X_FIRST = (slice(0, 1), slice(1, 2), slice(2, 4))
-X_LOADS = ((LEAD * P, 512, 512, 512), (512, 512, 1024))
+X_LOADS = ((LEAD * P, 512, 512, 512), (1024, 1024))
 ADJ_ROWS = 4
 PIECE_WIDTHS = (512, 512, 512, 320, 128, 64)
 WARM_UP_MATMULS = 13
@@ -38,11 +38,6 @@ def tile_netgraphconvolution_b_kernel(tc, x, adj, w, bias, base, offs, out):
         for blocks in W_FIRST:
             nc.scalar.dma_start(w_sb[:, blocks, :], w_view[:, blocks, :])
 
-        bias_loaded = held.tile([P, chan_blocks], F32, name="bias_loaded")
-        nc.gpsimd.dma_start(bias_loaded[:], bias.rearrange("(b p) o -> p (b o)", p=P))
-        bias_sb = held.tile([P, chan_blocks], F32, name="bias_sb")
-        nc.vector.tensor_copy(bias_sb[:], bias_loaded[:])
-
         x_view = x.rearrange("u (b p) m -> u p b m", p=P)
         x_block = {}
         for u in range(graphs):
@@ -57,6 +52,11 @@ def tile_netgraphconvolution_b_kernel(tc, x, adj, w, bias, base, offs, out):
                 for nb in range(start // P, (start + width) // P):
                     x_block[u, nb] = (x_sb, nb * P - start)
                 start += width
+
+        bias_loaded = held.tile([P, chan_blocks], F32, name="bias_loaded")
+        nc.sync.dma_start(bias_loaded[:], bias.rearrange("(b p) o -> p (b o)", p=P))
+        bias_sb = held.tile([P, chan_blocks], F32, name="bias_sb")
+        nc.vector.tensor_copy(bias_sb[:], bias_loaded[:])
 
         adj_view = adj.rearrange("(b p) j -> p b j", p=P)
         squared = {}

@@ -10,9 +10,7 @@ P = 128
 ALIGN = 512
 BANK = 512
 LEAD = 4
-W_FIRST = (slice(0, 1), slice(1, 4))
-X_FIRST = (slice(0, 1), slice(1, 2), slice(2, 4))
-X_LOADS = ((LEAD * P, 512, 512, 512), (1024, 1024))
+X_LOADS = ((512, 512, 512), (1024, 1024))
 ADJ_ROWS = 4
 PIECE_WIDTHS = (512, 512, 512, 320, 128, 64)
 WARM_UP_MATMULS = 13
@@ -35,20 +33,21 @@ def tile_netgraphconvolution_b_kernel(tc, x, adj, w, bias, base, offs, out):
     ):
         w_sb = held.tile([P, feat_blocks, chans], BF16, name="w_sb", align_bytes=ALIGN)
         w_view = w.rearrange("(b p) c -> p b c", p=P)
-        for blocks in W_FIRST:
-            nc.scalar.dma_start(w_sb[:, blocks, :], w_view[:, blocks, :])
 
         x_view = x.rearrange("u (b p) m -> u p b m", p=P)
-        x_block = {}
+        x_lead = held.tile([P, feat_blocks, LEAD * P], BF16, name="x_lead", align_bytes=ALIGN)
+        nc.sync.dma_start(w_sb[:, :1, :], w_view[:, :1, :])
+        nc.sync.dma_start(x_lead[:, :1, :], x_view[0, :, :1, : LEAD * P])
+        nc.sync.dma_start(w_sb[:, 1:, :], w_view[:, 1:, :])
+        nc.sync.dma_start(x_lead[:, 1:2, :], x_view[0, :, 1:2, : LEAD * P])
+        nc.sync.dma_start(x_lead[:, 2:, :], x_view[0, :, 2:, : LEAD * P])
+
+        x_block = {(0, nb): (x_lead, nb * P) for nb in range(LEAD)}
         for u in range(graphs):
-            start = 0
+            start = LEAD * P if u == 0 else 0
             for width in X_LOADS[u]:
                 x_sb = held.tile([P, feat_blocks, width], BF16, name=f"x{u}_{start}", align_bytes=ALIGN)
-                if u == 0 and start == 0:
-                    for blocks in X_FIRST:
-                        nc.sync.dma_start(x_sb[:, blocks, :], x_view[u, :, blocks, :width])
-                else:
-                    nc.sync.dma_start(x_sb[:], x_view[u, :, :, start : start + width])
+                nc.sync.dma_start(x_sb[:], x_view[u, :, :, start : start + width])
                 for nb in range(start // P, (start + width) // P):
                     x_block[u, nb] = (x_sb, nb * P - start)
                 start += width

import concourse.mybir as mybir

FLOPS = 2 * 2 * 512 * 2048 * 256 + 2 * 2048 * 2048 * 256

BF16, F32, U16 = mybir.dt.bfloat16, mybir.dt.float32, mybir.dt.uint16
ACT = mybir.ActivationFunctionType
ALU = mybir.AluOpType

P = 128
ALIGN = 512
BANK = 512
LEAD = 4
X_LOADS = ((512, 512, 512), (1024, 1024))
ADJ_ROWS = 4
PIECE_WIDTHS = (512, 512, 512, 320, 128, 64)
WARM_UP_MATMULS = 13


def tile_netgraphconvolution_b_kernel(tc, x, adj, w, bias, base, offs, out):
    nc = tc.nc
    graphs, feats, nodes = x.shape
    chans = w.shape[1]
    entries = adj.shape[1]
    slots = base.shape[1]
    feat_blocks, node_blocks, chan_blocks = feats // P, nodes // P, chans // P
    graph_entries = entries // graphs
    assert sum(PIECE_WIDTHS) == entries and graph_entries % BANK == 0

    with (
        tc.tile_pool(name="held", bufs=1) as held,
        tc.tile_pool(name="adj_ring", bufs=8) as adj_ring,
        tc.psum_pool(name="banks", bufs=8) as banks,
    ):
        w_sb = held.tile([P, feat_blocks, chans], BF16, name="w_sb", align_bytes=ALIGN)
        w_view = w.rearrange("(b p) c -> p b c", p=P)

        x_view = x.rearrange("u (b p) m -> u p b m", p=P)
        x_lead = held.tile([P, feat_blocks, LEAD * P], BF16, name="x_lead", align_bytes=ALIGN)
        nc.sync.dma_start(w_sb[:, :1, :], w_view[:, :1, :])
        nc.sync.dma_start(x_lead[:, :1, :], x_view[0, :, :1, : LEAD * P])
        nc.sync.dma_start(w_sb[:, 1:, :], w_view[:, 1:, :])
        nc.sync.dma_start(x_lead[:, 1:2, :], x_view[0, :, 1:2, : LEAD * P])
        nc.sync.dma_start(x_lead[:, 2:, :], x_view[0, :, 2:, : LEAD * P])

        x_block = {(0, nb): (x_lead, nb * P) for nb in range(LEAD)}
        for u in range(graphs):
            start = LEAD * P if u == 0 else 0
            for width in X_LOADS[u]:
                x_sb = held.tile([P, feat_blocks, width], BF16, name=f"x{u}_{start}", align_bytes=ALIGN)
                nc.sync.dma_start(x_sb[:], x_view[u, :, :, start : start + width])
                for nb in range(start // P, (start + width) // P):
                    x_block[u, nb] = (x_sb, nb * P - start)
                start += width

        bias_loaded = held.tile([P, chan_blocks], F32, name="bias_loaded")
        nc.sync.dma_start(bias_loaded[:], bias.rearrange("(b p) o -> p (b o)", p=P))
        bias_sb = held.tile([P, chan_blocks], F32, name="bias_sb")
        nc.vector.tensor_copy(bias_sb[:], bias_loaded[:])

        adj_view = adj.rearrange("(b p) j -> p b j", p=P)
        squared = {}
        for strip in range(entries // BANK):
            for g in range(node_blocks // ADJ_ROWS):
                raw = adj_ring.tile([P, ADJ_ROWS, BANK], BF16, name="raw", align_bytes=ALIGN)
                nc.sync.dma_start(
                    raw[:], adj_view[:, g * ADJ_ROWS : (g + 1) * ADJ_ROWS, strip * BANK : (strip + 1) * BANK]
                )
                squared[strip, g] = held.tile(
                    [P, ADJ_ROWS, BANK], BF16, name=f"squared{strip}_{g}", align_bytes=ALIGN
                )
                nc.vector.tensor_tensor(squared[strip, g][:], raw[:], raw[:], ALU.mult)

        offsets = held.tile([P, entries // 16], U16, name="offsets")
        nc.sync.dma_start(offsets[:], offs)

        window = []
        for cb in range(chan_blocks):
            window.append(held.tile([P, slots], F32, name=f"window{cb}", align_bytes=ALIGN))
            nc.sync.dma_start(window[cb][:], base[cb * P : (cb + 1) * P, :])

        zeros = held.tile([P, P], BF16, name="zeros", align_bytes=ALIGN)
        nc.vector.memset(zeros[:], 0.0)
        warm_bank = banks.tile([P, P], F32, name="warm_bank", tag="bank")
        for turn in range(WARM_UP_MATMULS):
            nc.tensor.matmul(warm_bank[:], zeros[:], zeros[:], start=True, stop=True)

        support = [
            held.tile([P, node_blocks, chans], BF16, name=f"support{u}", align_bytes=ALIGN) for u in range(graphs)
        ]
        lead_banks = [banks.tile([P, chans], F32, name=f"lead_bank{nb}", tag="bank") for nb in range(LEAD)]
        for fb in range(feat_blocks):
            for nb in range(LEAD):
                x_sb, col = x_block[0, nb]
                nc.tensor.matmul(
                    lead_banks[nb][:],
                    x_sb[:, fb, col : col + P],
                    w_sb[:, fb, :],
                    start=fb == 0,
                    stop=fb == feat_blocks - 1,
                )
        for nb in range(LEAD):
            nc.scalar.copy(support[0][:, nb, :], lead_banks[nb][:])
        for u in range(graphs):
            for pair in range(LEAD // 2 if u == 0 else 0, node_blocks // 2):
                bank = banks.tile([P, 2, chans], F32, name="bank", tag="bank")
                for half in range(2):
                    x_sb, col = x_block[u, 2 * pair + half]
                    for fb in range(feat_blocks):
                        nc.tensor.matmul(
                            bank[:, half, :],
                            x_sb[:, fb, col : col + P],
                            w_sb[:, fb, :],
                            start=fb == 0,
                            stop=fb == feat_blocks - 1,
                        )
                nc.scalar.copy(support[u][:, 2 * pair : 2 * pair + 2, :], bank[:])

        for cb in range(chan_blocks):
            above = held.tile([P, entries], F32, name=f"above{cb}", align_bytes=ALIGN)
            below = held.tile([P, entries], F32, name=f"below{cb}", align_bytes=ALIGN)
            first = 0
            last_block = cb == chan_blocks - 1
            for width in PIECE_WIDTHS if last_block else (BANK,) * (entries // BANK):
                u = first // graph_entries
                strip, col = divmod(first, BANK)
                assert col + width <= BANK
                v_bank = banks.tile([P, BANK], F32, name="v_bank", tag="bank")
                v = v_bank[:, :width]
                for nb in range(node_blocks):
                    g, row = divmod(nb, ADJ_ROWS)
                    nc.tensor.matmul(
                        v,
                        support[u][:, nb, cb * P : (cb + 1) * P],
                        squared[strip, g][:, row, col : col + width],
                        start=nb == 0,
                        stop=nb == node_blocks - 1,
                    )
                cols = slice(first, first + width)
                nc.scalar.activation(below[:, cols], v, ACT.Exp, bias=bias_sb[:, cb : cb + 1])
                nc.scalar.activation(above[:, cols], v, ACT.Relu, bias=bias_sb[:, cb : cb + 1])
                nc.vector.tensor_scalar(below[:, cols], below[:, cols], 1.0, -1.0, ALU.min, ALU.add)
                first += width

            nc.vector.tensor_tensor(window[cb][:].indirect(offsets[:]), above[:], below[:], ALU.add)
            nc.sync.dma_start(out[cb * P : (cb + 1) * P, :], window[cb][:])
